import numpy as np
import ml_dtypes

BF16 = ml_dtypes.bfloat16


def bf(x):
    return np.asarray(x, np.float32).astype(BF16)


def f32(x):
    return np.asarray(x, np.float32)


def f64(x):
    return np.asarray(x).astype(np.float64)


def striped(idx):
    return np.tile(idx.reshape(-1, 16).T, (8, 1))


C, S, N, D = 256, 512, 64, 64
LOG_2PI = np.log(2.0 * np.pi)


def setup_inputs():
    return {"base": f32(5.0 * np.random.standard_normal((C, S))), "x": f32(0.5 * np.random.standard_normal((C, D))), "means": f32(0.5 * np.random.standard_normal((C, N, D))), "offs": striped(np.random.permutation(S)[:N])}


def reference(base, x, means, offs):
    idx = offs[:16].T.reshape(-1)
    diff = f64(x)[:, None, :] - f64(means)
    out = f64(base).copy()
    out[:, idx] = -0.5 * np.sum(diff * diff, axis=-1) - 0.5 * D * LOG_2PI
    return out

@@ -1,0 +1,63 @@
+import math
+
+import concourse.mybir as mybir
+
+F32 = mybir.dt.float32
+U16 = mybir.dt.uint16
+ALU = mybir.AluOpType
+ACT = mybir.ActivationFunctionType
+
+P = 128
+SAMPLES, SLOTS, GAUSSIANS, VARIABLES = 256, 512, 64, 64
+BLOCKS = SAMPLES // P
+CHUNK = 16
+CHUNKS = GAUSSIANS // CHUNK
+LOG_NORM = -0.5 * VARIABLES * math.log(2.0 * math.pi)
+
+
+def tile_gaussiantensor_kernel(tc, base, x, means, offs, out):
+    nc = tc.nc
+    with (
+        tc.tile_pool(name="held", bufs=1) as held,
+        tc.tile_pool(name="block", bufs=BLOCKS) as block,
+        tc.tile_pool(name="loads", bufs=BLOCKS * CHUNKS) as loads,
+        tc.tile_pool(name="work", bufs=3) as work,
+    ):
+        offsets = held.tile([P, GAUSSIANS // 16], U16, name="offsets")
+        nc.sync.dma_start(offsets[:], offs)
+        log_norm = held.tile([P, GAUSSIANS], F32, name="log_norm")
+        nc.vector.memset(log_norm[:], LOG_NORM)
+
+        for b in range(BLOCKS):
+            rows = slice(b * P, (b + 1) * P)
+            sample = block.tile([P, VARIABLES], F32, name="sample")
+            nc.sync.dma_start(sample[:], x[rows, :])
+            window = block.tile([P, SLOTS], F32, name="window")
+            nc.sync.dma_start(window[:], base[rows, :])
+            exponent = block.tile([P, GAUSSIANS], F32, name="exponent")
+
+            for k in range(CHUNKS):
+                cols = slice(k * CHUNK, (k + 1) * CHUNK)
+                mean = loads.tile([P, CHUNK, VARIABLES], F32, name="mean")
+                nc.sync.dma_start(mean[:], means[rows, cols, :])
+                diff = work.tile([P, CHUNK, VARIABLES], F32, name="diff")
+                nc.vector.tensor_tensor(
+                    diff[:],
+                    mean[:],
+                    sample[:].unsqueeze(1).to_broadcast([P, CHUNK, VARIABLES]),
+                    ALU.subtract,
+                )
+                half_square = work.tile([P, CHUNK, VARIABLES], F32, name="half_square")
+                nc.scalar.activation(half_square[:], diff[:], ACT.Square, scale=math.sqrt(0.5))
+                nc.vector.tensor_reduce(
+                    exponent[:, cols],
+                    half_square[:],
+                    axis=mybir.AxisListType.X,
+                    op=ALU.add,
+                    negate=True,
+                )
+
+            nc.vector.tensor_tensor(
+                window[:].indirect(offsets[:]), exponent[:], log_norm[:], ALU.add
+            )
+            nc.sync.dma_start(out[rows, :], window[:])

@@ -1,6 +1,7 @@
 import math
 
 import concourse.mybir as mybir
+from concourse.masks import make_identity
 
 F32 = mybir.dt.float32
 U16 = mybir.dt.uint16
@@ -10,9 +11,12 @@ ACT = mybir.ActivationFunctionType
 P = 128
 SAMPLES, SLOTS, GAUSSIANS, VARIABLES = 256, 512, 64, 64
 BLOCKS = SAMPLES // P
-CHUNK = 16
-CHUNKS = GAUSSIANS // CHUNK
 LOG_NORM = -0.5 * VARIABLES * math.log(2.0 * math.pi)
+CHUNK = 16
+CHUNKS = SAMPLES // P * GAUSSIANS // CHUNK
+CHUNKS_IN_BLOCK = GAUSSIANS // CHUNK
+GPSIMD_SHARE = 7
+GROUP = 8
 
 
 def tile_gaussiantensor_kernel(tc, base, x, means, offs, out):
@@ -20,44 +24,83 @@ def tile_gaussiantensor_kernel(tc, base, x, means, offs, out):
     with (
         tc.tile_pool(name="held", bufs=1) as held,
         tc.tile_pool(name="block", bufs=BLOCKS) as block,
-        tc.tile_pool(name="loads", bufs=BLOCKS * CHUNKS) as loads,
-        tc.tile_pool(name="work", bufs=3) as work,
+        tc.tile_pool(name="loads", bufs=CHUNKS) as loads,
+        tc.tile_pool(name="work", bufs=CHUNKS) as work,
+        tc.psum_pool(name="psum", bufs=3) as psum,
     ):
         offsets = held.tile([P, GAUSSIANS // 16], U16, name="offsets")
         nc.sync.dma_start(offsets[:], offs)
         log_norm = held.tile([P, GAUSSIANS], F32, name="log_norm")
         nc.vector.memset(log_norm[:], LOG_NORM)
+        identity = held.tile([P, P], F32, name="identity")
+        make_identity(nc, identity[:])
+        scratch = held.tile([P, 1], F32, name="scratch")
+        nc.scalar.activation(scratch[:], log_norm[:, 0:1], ACT.Square)
 
+        samples, windows, exponents, chunks = [], [], [], []
         for b in range(BLOCKS):
             rows = slice(b * P, (b + 1) * P)
             sample = block.tile([P, VARIABLES], F32, name="sample")
             nc.sync.dma_start(sample[:], x[rows, :])
+            samples.append(sample)
+            for k in range(CHUNKS_IN_BLOCK):
+                mean = loads.tile([P, CHUNK, VARIABLES], F32, name="mean")
+                nc.sync.dma_start(mean[:], means[rows, k * CHUNK : (k + 1) * CHUNK, :])
+                chunks.append(mean)
             window = block.tile([P, SLOTS], F32, name="window")
             nc.sync.dma_start(window[:], base[rows, :])
+            windows.append(window)
             exponent = block.tile([P, GAUSSIANS], F32, name="exponent")
+            exponents.append(exponent)
 
-            for k in range(CHUNKS):
-                cols = slice(k * CHUNK, (k + 1) * CHUNK)
-                mean = loads.tile([P, CHUNK, VARIABLES], F32, name="mean")
-                nc.sync.dma_start(mean[:], means[rows, cols, :])
-                diff = work.tile([P, CHUNK, VARIABLES], F32, name="diff")
-                nc.vector.tensor_tensor(
-                    diff[:],
-                    mean[:],
-                    sample[:].unsqueeze(1).to_broadcast([P, CHUNK, VARIABLES]),
+        def subtract(i):
+            diff = work.tile([P, CHUNK, VARIABLES], F32, name="diff")
+            for engine, first, last in (
+                (nc.gpsimd, 0, GPSIMD_SHARE),
+                (nc.vector, GPSIMD_SHARE, CHUNK),
+            ):
+                engine.tensor_tensor(
+                    diff[:, first:last, :],
+                    chunks[i][:, first:last, :],
+                    samples[i // CHUNKS_IN_BLOCK][:]
+                    .unsqueeze(1)
+                    .to_broadcast([P, last - first, VARIABLES]),
                     ALU.subtract,
                 )
-                half_square = work.tile([P, CHUNK, VARIABLES], F32, name="half_square")
-                nc.scalar.activation(half_square[:], diff[:], ACT.Square, scale=math.sqrt(0.5))
-                nc.vector.tensor_reduce(
-                    exponent[:, cols],
-                    half_square[:],
-                    axis=mybir.AxisListType.X,
-                    op=ALU.add,
-                    negate=True,
-                )
+            return diff
 
-            nc.vector.tensor_tensor(
-                window[:].indirect(offsets[:]), exponent[:], log_norm[:], ALU.add
+        def square_and_sum(i, diff):
+            half_square = work.tile([P, CHUNK, VARIABLES], F32, name="half_square")
+            nc.scalar.activation(half_square[:], diff[:], ACT.Square, scale=math.sqrt(0.5))
+            summands = half_square
+            if i % 2 == 0 and i + 2 < CHUNKS:
+                summands = psum.tile([P, CHUNK, GROUP], F32, name="partial")
+                groups = VARIABLES // GROUP
+                for g in range(groups):
+                    nc.tensor.matmul(
+                        summands[:],
+                        identity[:],
+                        half_square[:, :, g * GROUP : (g + 1) * GROUP],
+                        start=(g == 0),
+                        stop=(g == groups - 1),
+                    )
+            k = i % CHUNKS_IN_BLOCK
+            nc.vector.tensor_reduce(
+                exponents[i // CHUNKS_IN_BLOCK][:, k * CHUNK : (k + 1) * CHUNK],
+                summands[:],
+                axis=mybir.AxisListType.X,
+                op=ALU.add,
+                negate=True,
             )
-            nc.sync.dma_start(out[rows, :], window[:])
+
+        diffs = [subtract(0)]
+        for i in range(CHUNKS):
+            if i + 1 < CHUNKS:
+                diffs.append(subtract(i + 1))
+            square_and_sum(i, diffs[i])
+            if (i + 1) % CHUNKS_IN_BLOCK == 0:
+                b = i // CHUNKS_IN_BLOCK
+                nc.vector.tensor_tensor(
+                    windows[b][:].indirect(offsets[:]), exponents[b][:], log_norm[:], ALU.add
+                )
+                nc.sync.dma_start(out[b * P : (b + 1) * P, :], windows[b][:])

@@ -27,6 +27,7 @@ def tile_gaussiantensor_kernel(tc, base, x, means, offs, out):
         tc.tile_pool(name="loads", bufs=CHUNKS) as loads,
         tc.tile_pool(name="work", bufs=CHUNKS) as work,
         tc.psum_pool(name="psum", bufs=3) as psum,
+        tc.psum_pool(name="psum_block", bufs=BLOCKS) as psum_block,
     ):
         offsets = held.tile([P, GAUSSIANS // 16], U16, name="offsets")
         nc.sync.dma_start(offsets[:], offs)
@@ -37,12 +38,15 @@ def tile_gaussiantensor_kernel(tc, base, x, means, offs, out):
         scratch = held.tile([P, 1], F32, name="scratch")
         nc.scalar.activation(scratch[:], log_norm[:, 0:1], ACT.Square)
 
-        samples, windows, exponents, chunks = [], [], [], []
+        samples, samples_psum, windows, exponents, chunks = [], [], [], [], []
         for b in range(BLOCKS):
             rows = slice(b * P, (b + 1) * P)
             sample = block.tile([P, VARIABLES], F32, name="sample")
             nc.sync.dma_start(sample[:], x[rows, :])
             samples.append(sample)
+            sample_psum = psum_block.tile([P, VARIABLES], F32, name="sample_psum")
+            nc.tensor.matmul(sample_psum[:], identity[:], sample[:], start=True, stop=True)
+            samples_psum.append(sample_psum)
             for k in range(CHUNKS_IN_BLOCK):
                 mean = loads.tile([P, CHUNK, VARIABLES], F32, name="mean")
                 nc.sync.dma_start(mean[:], means[rows, k * CHUNK : (k + 1) * CHUNK, :])
@@ -55,16 +59,15 @@ def tile_gaussiantensor_kernel(tc, base, x, means, offs, out):
 
         def subtract(i):
             diff = work.tile([P, CHUNK, VARIABLES], F32, name="diff")
-            for engine, first, last in (
-                (nc.gpsimd, 0, GPSIMD_SHARE),
-                (nc.vector, GPSIMD_SHARE, CHUNK),
+            b = i // CHUNKS_IN_BLOCK
+            for engine, sample, first, last in (
+                (nc.gpsimd, samples[b], 0, GPSIMD_SHARE),
+                (nc.vector, samples_psum[b], GPSIMD_SHARE, CHUNK),
             ):
                 engine.tensor_tensor(
                     diff[:, first:last, :],
                     chunks[i][:, first:last, :],
-                    samples[i // CHUNKS_IN_BLOCK][:]
-                    .unsqueeze(1)
-                    .to_broadcast([P, last - first, VARIABLES]),
+                    sample[:].unsqueeze(1).to_broadcast([P, last - first, VARIABLES]),
                     ALU.subtract,
                 )
             return diff

@@ -13,8 +13,8 @@ SAMPLES, SLOTS, GAUSSIANS, VARIABLES = 256, 512, 64, 64
 BLOCKS = SAMPLES // P
 LOG_NORM = -0.5 * VARIABLES * math.log(2.0 * math.pi)
 CHUNK = 16
-CHUNKS = SAMPLES // P * GAUSSIANS // CHUNK
 CHUNKS_IN_BLOCK = GAUSSIANS // CHUNK
+CHUNKS = BLOCKS * CHUNKS_IN_BLOCK
 GPSIMD_SHARE = 7
 GROUP = 8
 
@@ -24,9 +24,8 @@ def tile_gaussiantensor_kernel(tc, base, x, means, offs, out):
     with (
         tc.tile_pool(name="held", bufs=1) as held,
         tc.tile_pool(name="block", bufs=BLOCKS) as block,
-        tc.tile_pool(name="loads", bufs=CHUNKS) as loads,
-        tc.tile_pool(name="work", bufs=CHUNKS) as work,
-        tc.psum_pool(name="psum", bufs=3) as psum,
+        tc.tile_pool(name="chunk", bufs=CHUNKS) as chunk,
+        tc.psum_pool(name="psum", bufs=4) as psum,
         tc.psum_pool(name="psum_block", bufs=BLOCKS) as psum_block,
     ):
         offsets = held.tile([P, GAUSSIANS // 16], U16, name="offsets")
@@ -38,19 +37,20 @@ def tile_gaussiantensor_kernel(tc, base, x, means, offs, out):
         scratch = held.tile([P, 1], F32, name="scratch")
         nc.scalar.activation(scratch[:], log_norm[:, 0:1], ACT.Square)
 
-        samples, samples_psum, windows, exponents, chunks = [], [], [], [], []
+        samples, samples_psum, windows, exponents, loaded = [], [], [], [], []
         for b in range(BLOCKS):
-            rows = slice(b * P, (b + 1) * P)
             sample = block.tile([P, VARIABLES], F32, name="sample")
-            nc.sync.dma_start(sample[:], x[rows, :])
+            nc.sync.dma_start(sample[:], x[b * P : (b + 1) * P, :])
             samples.append(sample)
             sample_psum = psum_block.tile([P, VARIABLES], F32, name="sample_psum")
             nc.tensor.matmul(sample_psum[:], identity[:], sample[:], start=True, stop=True)
             samples_psum.append(sample_psum)
+        for b in range(BLOCKS):
+            rows = slice(b * P, (b + 1) * P)
             for k in range(CHUNKS_IN_BLOCK):
-                mean = loads.tile([P, CHUNK, VARIABLES], F32, name="mean")
+                mean = chunk.tile([P, CHUNK, VARIABLES], F32, name="mean")
                 nc.sync.dma_start(mean[:], means[rows, k * CHUNK : (k + 1) * CHUNK, :])
-                chunks.append(mean)
+                loaded.append(mean)
             window = block.tile([P, SLOTS], F32, name="window")
             nc.sync.dma_start(window[:], base[rows, :])
             windows.append(window)
@@ -58,7 +58,7 @@ def tile_gaussiantensor_kernel(tc, base, x, means, offs, out):
             exponents.append(exponent)
 
         def subtract(i):
-            diff = work.tile([P, CHUNK, VARIABLES], F32, name="diff")
+            diff = chunk.tile([P, CHUNK, VARIABLES], F32, name="diff")
             b = i // CHUNKS_IN_BLOCK
             for engine, sample, first, last in (
                 (nc.gpsimd, samples[b], 0, GPSIMD_SHARE),
@@ -66,27 +66,13 @@ def tile_gaussiantensor_kernel(tc, base, x, means, offs, out):
             ):
                 engine.tensor_tensor(
                     diff[:, first:last, :],
-                    chunks[i][:, first:last, :],
+                    loaded[i][:, first:last, :],
                     sample[:].unsqueeze(1).to_broadcast([P, last - first, VARIABLES]),
                     ALU.subtract,
                 )
             return diff
 
-        def square_and_sum(i, diff):
-            half_square = work.tile([P, CHUNK, VARIABLES], F32, name="half_square")
-            nc.scalar.activation(half_square[:], diff[:], ACT.Square, scale=math.sqrt(0.5))
-            summands = half_square
-            if i % 2 == 0 and i + 2 < CHUNKS:
-                summands = psum.tile([P, CHUNK, GROUP], F32, name="partial")
-                groups = VARIABLES // GROUP
-                for g in range(groups):
-                    nc.tensor.matmul(
-                        summands[:],
-                        identity[:],
-                        half_square[:, :, g * GROUP : (g + 1) * GROUP],
-                        start=(g == 0),
-                        stop=(g == groups - 1),
-                    )
+        def negated_sum(i, summands):
             k = i % CHUNKS_IN_BLOCK
             nc.vector.tensor_reduce(
                 exponents[i // CHUNKS_IN_BLOCK][:, k * CHUNK : (k + 1) * CHUNK],
@@ -96,14 +82,34 @@ def tile_gaussiantensor_kernel(tc, base, x, means, offs, out):
                 negate=True,
             )
 
+        def square_and_sum(i, diff):
+            half_square = chunk.tile([P, CHUNK, VARIABLES], F32, name="half_square")
+            nc.scalar.activation(half_square[:], diff[:], ACT.Square, scale=math.sqrt(0.5))
+            if i % 2 == 0:
+                partial = psum.tile([P, CHUNK, GROUP], F32, name="partial")
+                groups = VARIABLES // GROUP
+                for g in range(groups):
+                    nc.tensor.matmul(
+                        partial[:],
+                        identity[:],
+                        half_square[:, :, g * GROUP : (g + 1) * GROUP],
+                        start=(g == 0),
+                        stop=(g == groups - 1),
+                    )
+                negated_sum(i, partial)
+            else:
+                negated_sum(i, half_square)
+
+        def finish(b):
+            nc.vector.tensor_tensor(
+                windows[b][:].indirect(offsets[:]), exponents[b][:], log_norm[:], ALU.add
+            )
+            nc.sync.dma_start(out[b * P : (b + 1) * P, :], windows[b][:])
+
         diffs = [subtract(0)]
         for i in range(CHUNKS):
             if i + 1 < CHUNKS:
                 diffs.append(subtract(i + 1))
             square_and_sum(i, diffs[i])
             if (i + 1) % CHUNKS_IN_BLOCK == 0:
-                b = i // CHUNKS_IN_BLOCK
-                nc.vector.tensor_tensor(
-                    windows[b][:].indirect(offsets[:]), exponents[b][:], log_norm[:], ALU.add
-                )
-                nc.sync.dma_start(out[b * P : (b + 1) * P, :], windows[b][:])
+                finish(i // CHUNKS_IN_BLOCK)

@@ -15,8 +15,8 @@ LOG_NORM = -0.5 * VARIABLES * math.log(2.0 * math.pi)
 CHUNK = 16
 CHUNKS_IN_BLOCK = GAUSSIANS // CHUNK
 CHUNKS = BLOCKS * CHUNKS_IN_BLOCK
-GPSIMD_SHARE = 7
 GROUP = 8
+GPSIMD_SHARE = 7
 
 
 def tile_gaussiantensor_kernel(tc, base, x, means, offs, out):
@@ -25,7 +25,7 @@ def tile_gaussiantensor_kernel(tc, base, x, means, offs, out):
         tc.tile_pool(name="held", bufs=1) as held,
         tc.tile_pool(name="block", bufs=BLOCKS) as block,
         tc.tile_pool(name="chunk", bufs=CHUNKS) as chunk,
-        tc.psum_pool(name="psum", bufs=4) as psum,
+        tc.psum_pool(name="psum", bufs=CHUNKS // 2) as psum,
         tc.psum_pool(name="psum_block", bufs=BLOCKS) as psum_block,
     ):
         offsets = held.tile([P, GAUSSIANS // 16], U16, name="offsets")
@@ -37,14 +37,14 @@ def tile_gaussiantensor_kernel(tc, base, x, means, offs, out):
         scratch = held.tile([P, 1], F32, name="scratch")
         nc.scalar.activation(scratch[:], log_norm[:, 0:1], ACT.Square)
 
-        samples, samples_psum, windows, exponents, loaded = [], [], [], [], []
+        x_sbuf, x_psum, windows, exponents, loaded = [], [], [], [], []
         for b in range(BLOCKS):
             sample = block.tile([P, VARIABLES], F32, name="sample")
             nc.sync.dma_start(sample[:], x[b * P : (b + 1) * P, :])
-            samples.append(sample)
+            x_sbuf.append(sample)
             sample_psum = psum_block.tile([P, VARIABLES], F32, name="sample_psum")
             nc.tensor.matmul(sample_psum[:], identity[:], sample[:], start=True, stop=True)
-            samples_psum.append(sample_psum)
+            x_psum.append(sample_psum)
         for b in range(BLOCKS):
             rows = slice(b * P, (b + 1) * P)
             for k in range(CHUNKS_IN_BLOCK):
@@ -57,59 +57,46 @@ def tile_gaussiantensor_kernel(tc, base, x, means, offs, out):
             exponent = block.tile([P, GAUSSIANS], F32, name="exponent")
             exponents.append(exponent)
 
-        def subtract(i):
+        for i in range(CHUNKS):
+            b, k = divmod(i, CHUNKS_IN_BLOCK)
+
             diff = chunk.tile([P, CHUNK, VARIABLES], F32, name="diff")
-            b = i // CHUNKS_IN_BLOCK
-            for engine, sample, first, last in (
-                (nc.gpsimd, samples[b], 0, GPSIMD_SHARE),
-                (nc.vector, samples_psum[b], GPSIMD_SHARE, CHUNK),
+            for engine, x_tile, first, last in (
+                (nc.gpsimd, x_sbuf[b], 0, GPSIMD_SHARE),
+                (nc.vector, x_psum[b], GPSIMD_SHARE, CHUNK),
             ):
                 engine.tensor_tensor(
                     diff[:, first:last, :],
                     loaded[i][:, first:last, :],
-                    sample[:].unsqueeze(1).to_broadcast([P, last - first, VARIABLES]),
+                    x_tile[:].unsqueeze(1).to_broadcast([P, last - first, VARIABLES]),
                     ALU.subtract,
                 )
-            return diff
 
-        def negated_sum(i, summands):
-            k = i % CHUNKS_IN_BLOCK
+            half_square = chunk.tile([P, CHUNK, VARIABLES], F32, name="half_square")
+            nc.scalar.activation(half_square[:], diff[:], ACT.Square, scale=math.sqrt(0.5))
+
+            summands = half_square
+            if i % 2 == 0:
+                summands = psum.tile([P, CHUNK, GROUP], F32, name="partial")
+                groups = VARIABLES // GROUP
+                for g in range(groups):
+                    nc.tensor.matmul(
+                        summands[:],
+                        identity[:],
+                        half_square[:, :, g * GROUP : (g + 1) * GROUP],
+                        start=(g == 0),
+                        stop=(g == groups - 1),
+                    )
             nc.vector.tensor_reduce(
-                exponents[i // CHUNKS_IN_BLOCK][:, k * CHUNK : (k + 1) * CHUNK],
+                exponents[b][:, k * CHUNK : (k + 1) * CHUNK],
                 summands[:],
                 axis=mybir.AxisListType.X,
                 op=ALU.add,
                 negate=True,
             )
 
-        def square_and_sum(i, diff):
-            half_square = chunk.tile([P, CHUNK, VARIABLES], F32, name="half_square")
-            nc.scalar.activation(half_square[:], diff[:], ACT.Square, scale=math.sqrt(0.5))
-            if i % 2 == 0:
-                partial = psum.tile([P, CHUNK, GROUP], F32, name="partial")
-                groups = VARIABLES // GROUP
-                for g in range(groups):
-                    nc.tensor.matmul(
-                        partial[:],
-                        identity[:],
-                        half_square[:, :, g * GROUP : (g + 1) * GROUP],
-                        start=(g == 0),
-                        stop=(g == groups - 1),
-                    )
-                negated_sum(i, partial)
-            else:
-                negated_sum(i, half_square)
-
-        def finish(b):
-            nc.vector.tensor_tensor(
-                windows[b][:].indirect(offsets[:]), exponents[b][:], log_norm[:], ALU.add
-            )
-            nc.sync.dma_start(out[b * P : (b + 1) * P, :], windows[b][:])
-
-        diffs = [subtract(0)]
-        for i in range(CHUNKS):
-            if i + 1 < CHUNKS:
-                diffs.append(subtract(i + 1))
-            square_and_sum(i, diffs[i])
-            if (i + 1) % CHUNKS_IN_BLOCK == 0:
-                finish(i // CHUNKS_IN_BLOCK)
+            if k == CHUNKS_IN_BLOCK - 1:
+                nc.vector.tensor_tensor(
+                    windows[b][:].indirect(offsets[:]), exponents[b][:], log_norm[:], ALU.add
+                )
+                nc.sync.dma_start(out[b * P : (b + 1) * P, :], windows[b][:])

@@ -34,8 +34,6 @@ def tile_gaussiantensor_kernel(tc, base, x, means, offs, out):
         nc.vector.memset(log_norm[:], LOG_NORM)
         identity = held.tile([P, P], F32, name="identity")
         make_identity(nc, identity[:])
-        scratch = held.tile([P, 1], F32, name="scratch")
-        nc.scalar.activation(scratch[:], log_norm[:, 0:1], ACT.Square)
 
         x_sbuf, x_psum, windows, exponents, loaded = [], [], [], [], []
         for b in range(BLOCKS):
@@ -60,7 +58,17 @@ def tile_gaussiantensor_kernel(tc, base, x, means, offs, out):
         for i in range(CHUNKS):
             b, k = divmod(i, CHUNKS_IN_BLOCK)
 
+            def negated_sum(first, last, summands):
+                nc.vector.tensor_reduce(
+                    exponents[b][:, k * CHUNK + first : k * CHUNK + last],
+                    summands,
+                    axis=mybir.AxisListType.X,
+                    op=ALU.add,
+                    negate=True,
+                )
+
             diff = chunk.tile([P, CHUNK, VARIABLES], F32, name="diff")
+            half_square = chunk.tile([P, CHUNK, VARIABLES], F32, name="half_square")
             for engine, x_tile, first, last in (
                 (nc.gpsimd, x_sbuf[b], 0, GPSIMD_SHARE),
                 (nc.vector, x_psum[b], GPSIMD_SHARE, CHUNK),
@@ -71,29 +79,27 @@ def tile_gaussiantensor_kernel(tc, base, x, means, offs, out):
                     x_tile[:].unsqueeze(1).to_broadcast([P, last - first, VARIABLES]),
                     ALU.subtract,
                 )
+                nc.scalar.activation(
+                    half_square[:, first:last, :],
+                    diff[:, first:last, :],
+                    ACT.Square,
+                    scale=math.sqrt(0.5),
+                )
+                if i % 2 == 1:
+                    negated_sum(first, last, half_square[:, first:last, :])
 
-            half_square = chunk.tile([P, CHUNK, VARIABLES], F32, name="half_square")
-            nc.scalar.activation(half_square[:], diff[:], ACT.Square, scale=math.sqrt(0.5))
-
-            summands = half_square
             if i % 2 == 0:
-                summands = psum.tile([P, CHUNK, GROUP], F32, name="partial")
+                partial = psum.tile([P, CHUNK, GROUP], F32, name="partial")
                 groups = VARIABLES // GROUP
                 for g in range(groups):
                     nc.tensor.matmul(
-                        summands[:],
+                        partial[:],
                         identity[:],
                         half_square[:, :, g * GROUP : (g + 1) * GROUP],
                         start=(g == 0),
                         stop=(g == groups - 1),
                     )
-            nc.vector.tensor_reduce(
-                exponents[b][:, k * CHUNK : (k + 1) * CHUNK],
-                summands[:],
-                axis=mybir.AxisListType.X,
-                op=ALU.add,
-                negate=True,
-            )
+                negated_sum(0, CHUNK, partial[:])
 
             if k == CHUNKS_IN_BLOCK - 1:
                 nc.vector.tensor_tensor(

@@ -4,6 +4,7 @@ import concourse.mybir as mybir
 from concourse.masks import make_identity
 
 F32 = mybir.dt.float32
+BF16 = mybir.dt.bfloat16
 U16 = mybir.dt.uint16
 ALU = mybir.AluOpType
 ACT = mybir.ActivationFunctionType
@@ -13,10 +14,15 @@ SAMPLES, SLOTS, GAUSSIANS, VARIABLES = 256, 512, 64, 64
 BLOCKS = SAMPLES // P
 LOG_NORM = -0.5 * VARIABLES * math.log(2.0 * math.pi)
 CHUNK = 16
-CHUNKS_IN_BLOCK = GAUSSIANS // CHUNK
-CHUNKS = BLOCKS * CHUNKS_IN_BLOCK
+SMALL = 4
+CHUNKS_OF_BLOCK = (
+    (SMALL, CHUNK - SMALL, CHUNK, CHUNK, CHUNK),
+    (CHUNK, CHUNK, CHUNK, CHUNK - SMALL, SMALL),
+)
+CHUNKS = sum(len(sizes) for sizes in CHUNKS_OF_BLOCK)
 GROUP = 8
-GPSIMD_SHARE = 7
+GPSIMD_SHARE = 5
+PSUM_BANKS = 8
 
 
 def tile_gaussiantensor_kernel(tc, base, x, means, offs, out):
@@ -25,7 +31,7 @@ def tile_gaussiantensor_kernel(tc, base, x, means, offs, out):
         tc.tile_pool(name="held", bufs=1) as held,
         tc.tile_pool(name="block", bufs=BLOCKS) as block,
         tc.tile_pool(name="chunk", bufs=CHUNKS) as chunk,
-        tc.psum_pool(name="psum", bufs=CHUNKS // 2) as psum,
+        tc.psum_pool(name="psum", bufs=PSUM_BANKS - BLOCKS) as psum,
         tc.psum_pool(name="psum_block", bufs=BLOCKS) as psum_block,
     ):
         offsets = held.tile([P, GAUSSIANS // 16], U16, name="offsets")
@@ -34,6 +40,8 @@ def tile_gaussiantensor_kernel(tc, base, x, means, offs, out):
         nc.vector.memset(log_norm[:], LOG_NORM)
         identity = held.tile([P, P], F32, name="identity")
         make_identity(nc, identity[:])
+        identity_bf16 = held.tile([P, P], BF16, name="identity_bf16")
+        make_identity(nc, identity_bf16[:])
 
         x_sbuf, x_psum, windows, exponents, loaded = [], [], [], [], []
         for b in range(BLOCKS):
@@ -44,64 +52,64 @@ def tile_gaussiantensor_kernel(tc, base, x, means, offs, out):
             nc.tensor.matmul(sample_psum[:], identity[:], sample[:], start=True, stop=True)
             x_psum.append(sample_psum)
         for b in range(BLOCKS):
-            rows = slice(b * P, (b + 1) * P)
-            for k in range(CHUNKS_IN_BLOCK):
-                mean = chunk.tile([P, CHUNK, VARIABLES], F32, name="mean")
-                nc.sync.dma_start(mean[:], means[rows, k * CHUNK : (k + 1) * CHUNK, :])
-                loaded.append(mean)
+            first = 0
+            for size in CHUNKS_OF_BLOCK[b]:
+                mean = chunk.tile([P, size, VARIABLES], F32, name="mean")
+                nc.sync.dma_start(mean[:], means[b * P : (b + 1) * P, first : first + size, :])
+                loaded.append((b, first, size, mean))
+                first += size
+        for b in range(BLOCKS):
             window = block.tile([P, SLOTS], F32, name="window")
-            nc.sync.dma_start(window[:], base[rows, :])
+            nc.sync.dma_start(window[:], base[b * P : (b + 1) * P, :])
             windows.append(window)
             exponent = block.tile([P, GAUSSIANS], F32, name="exponent")
             exponents.append(exponent)
 
-        for i in range(CHUNKS):
-            b, k = divmod(i, CHUNKS_IN_BLOCK)
-
-            def negated_sum(first, last, summands):
-                nc.vector.tensor_reduce(
-                    exponents[b][:, k * CHUNK + first : k * CHUNK + last],
-                    summands,
-                    axis=mybir.AxisListType.X,
-                    op=ALU.add,
-                    negate=True,
-                )
-
-            diff = chunk.tile([P, CHUNK, VARIABLES], F32, name="diff")
-            half_square = chunk.tile([P, CHUNK, VARIABLES], F32, name="half_square")
-            for engine, x_tile, first, last in (
-                (nc.gpsimd, x_sbuf[b], 0, GPSIMD_SHARE),
-                (nc.vector, x_psum[b], GPSIMD_SHARE, CHUNK),
+        for b, first, size, mean in loaded:
+            diff = chunk.tile([P, size, VARIABLES], F32, name="diff")
+            half_square = chunk.tile([P, size, VARIABLES], BF16, name="half_square")
+            vector_share = size if size == SMALL else size - size * GPSIMD_SHARE // CHUNK
+            for engine, x_tile, lo, hi in (
+                (nc.vector, x_psum[b], 0, vector_share),
+                (nc.gpsimd, x_sbuf[b], vector_share, size),
             ):
+                if lo == hi:
+                    continue
                 engine.tensor_tensor(
-                    diff[:, first:last, :],
-                    loaded[i][:, first:last, :],
-                    x_tile[:].unsqueeze(1).to_broadcast([P, last - first, VARIABLES]),
+                    diff[:, lo:hi, :],
+                    mean[:, lo:hi, :],
+                    x_tile[:].unsqueeze(1).to_broadcast([P, hi - lo, VARIABLES]),
                     ALU.subtract,
                 )
                 nc.scalar.activation(
-                    half_square[:, first:last, :],
-                    diff[:, first:last, :],
+                    half_square[:, lo:hi, :],
+                    diff[:, lo:hi, :],
                     ACT.Square,
                     scale=math.sqrt(0.5),
                 )
-                if i % 2 == 1:
-                    negated_sum(first, last, half_square[:, first:last, :])
 
-            if i % 2 == 0:
-                partial = psum.tile([P, CHUNK, GROUP], F32, name="partial")
+            if size == SMALL:
+                summands = half_square
+            else:
+                summands = psum.tile([P, size, GROUP], F32, name="partial")
                 groups = VARIABLES // GROUP
                 for g in range(groups):
                     nc.tensor.matmul(
-                        partial[:],
-                        identity[:],
+                        summands[:],
+                        identity_bf16[:],
                         half_square[:, :, g * GROUP : (g + 1) * GROUP],
                         start=(g == 0),
                         stop=(g == groups - 1),
                     )
-                negated_sum(0, CHUNK, partial[:])
+            nc.vector.tensor_reduce(
+                exponents[b][:, first : first + size],
+                summands[:],
+                axis=mybir.AxisListType.X,
+                op=ALU.add,
+                negate=True,
+            )
 
-            if k == CHUNKS_IN_BLOCK - 1:
+            if first + size == GAUSSIANS:
                 nc.vector.tensor_tensor(
                     windows[b][:].indirect(offsets[:]), exponents[b][:], log_norm[:], ALU.add
                 )

@@ -14,14 +14,12 @@ SAMPLES, SLOTS, GAUSSIANS, VARIABLES = 256, 512, 64, 64
 BLOCKS = SAMPLES // P
 LOG_NORM = -0.5 * VARIABLES * math.log(2.0 * math.pi)
 CHUNK = 16
-SMALL = 4
-CHUNKS_OF_BLOCK = (
-    (SMALL, CHUNK - SMALL, CHUNK, CHUNK, CHUNK),
-    (CHUNK, CHUNK, CHUNK, CHUNK - SMALL, SMALL),
-)
-CHUNKS = sum(len(sizes) for sizes in CHUNKS_OF_BLOCK)
+CHUNKS_IN_BLOCK = GAUSSIANS // CHUNK
+CHUNKS = BLOCKS * CHUNKS_IN_BLOCK
+LOAD = 8
 GROUP = 8
 GPSIMD_SHARE = 5
+SMALL = 4
 PSUM_BANKS = 8
 
 
@@ -30,6 +28,7 @@ def tile_gaussiantensor_kernel(tc, base, x, means, offs, out):
     with (
         tc.tile_pool(name="held", bufs=1) as held,
         tc.tile_pool(name="block", bufs=BLOCKS) as block,
+        tc.tile_pool(name="load", bufs=CHUNKS * CHUNK // LOAD) as load,
         tc.tile_pool(name="chunk", bufs=CHUNKS) as chunk,
         tc.psum_pool(name="psum", bufs=PSUM_BANKS - BLOCKS) as psum,
         tc.psum_pool(name="psum_block", bufs=BLOCKS) as psum_block,
@@ -52,12 +51,10 @@ def tile_gaussiantensor_kernel(tc, base, x, means, offs, out):
             nc.tensor.matmul(sample_psum[:], identity[:], sample[:], start=True, stop=True)
             x_psum.append(sample_psum)
         for b in range(BLOCKS):
-            first = 0
-            for size in CHUNKS_OF_BLOCK[b]:
-                mean = chunk.tile([P, size, VARIABLES], F32, name="mean")
-                nc.sync.dma_start(mean[:], means[b * P : (b + 1) * P, first : first + size, :])
-                loaded.append((b, first, size, mean))
-                first += size
+            for first in range(0, GAUSSIANS, LOAD):
+                mean = load.tile([P, LOAD, VARIABLES], F32, name="mean")
+                nc.sync.dma_start(mean[:], means[b * P : (b + 1) * P, first : first + LOAD, :])
+                loaded.append(mean)
         for b in range(BLOCKS):
             window = block.tile([P, SLOTS], F32, name="window")
             nc.sync.dma_start(window[:], base[b * P : (b + 1) * P, :])
@@ -65,19 +62,34 @@ def tile_gaussiantensor_kernel(tc, base, x, means, offs, out):
             exponent = block.tile([P, GAUSSIANS], F32, name="exponent")
             exponents.append(exponent)
 
-        for b, first, size, mean in loaded:
-            diff = chunk.tile([P, size, VARIABLES], F32, name="diff")
-            half_square = chunk.tile([P, size, VARIABLES], BF16, name="half_square")
-            vector_share = size if size == SMALL else size - size * GPSIMD_SHARE // CHUNK
-            for engine, x_tile, lo, hi in (
-                (nc.vector, x_psum[b], 0, vector_share),
-                (nc.gpsimd, x_sbuf[b], vector_share, size),
-            ):
-                if lo == hi:
-                    continue
+        for i in range(CHUNKS):
+            b, k = divmod(i, CHUNKS_IN_BLOCK)
+            last_chunk = i == CHUNKS - 1
+
+            def negated_sum(lo, hi, summands):
+                nc.vector.tensor_reduce(
+                    exponents[b][:, k * CHUNK + lo : k * CHUNK + hi],
+                    summands,
+                    axis=mybir.AxisListType.X,
+                    op=ALU.add,
+                    negate=True,
+                )
+
+            if last_chunk:
+                pieces = [(nc.vector, x_psum[b], lo, lo + SMALL) for lo in range(0, CHUNK, SMALL)]
+            else:
+                pieces = [
+                    (nc.vector, x_psum[b], 0, LOAD),
+                    (nc.vector, x_psum[b], LOAD, CHUNK - GPSIMD_SHARE),
+                    (nc.gpsimd, x_sbuf[b], CHUNK - GPSIMD_SHARE, CHUNK),
+                ]
+            diff = chunk.tile([P, CHUNK, VARIABLES], F32, name="diff")
+            half_square = chunk.tile([P, CHUNK, VARIABLES], BF16, name="half_square")
+            for engine, x_tile, lo, hi in pieces:
+                mean = loaded[(i * CHUNK + lo) // LOAD]
                 engine.tensor_tensor(
                     diff[:, lo:hi, :],
-                    mean[:, lo:hi, :],
+                    mean[:, lo % LOAD : lo % LOAD + hi - lo, :],
                     x_tile[:].unsqueeze(1).to_broadcast([P, hi - lo, VARIABLES]),
                     ALU.subtract,
                 )
@@ -87,29 +99,23 @@ def tile_gaussiantensor_kernel(tc, base, x, means, offs, out):
                     ACT.Square,
                     scale=math.sqrt(0.5),
                 )
+                if last_chunk:
+                    negated_sum(lo, hi, half_square[:, lo:hi, :])
 
-            if size == SMALL:
-                summands = half_square
-            else:
-                summands = psum.tile([P, size, GROUP], F32, name="partial")
+            if not last_chunk:
+                partial = psum.tile([P, CHUNK, GROUP], F32, name="partial")
                 groups = VARIABLES // GROUP
                 for g in range(groups):
                     nc.tensor.matmul(
-                        summands[:],
+                        partial[:],
                         identity_bf16[:],
                         half_square[:, :, g * GROUP : (g + 1) * GROUP],
                         start=(g == 0),
                         stop=(g == groups - 1),
                     )
-            nc.vector.tensor_reduce(
-                exponents[b][:, first : first + size],
-                summands[:],
-                axis=mybir.AxisListType.X,
-                op=ALU.add,
-                negate=True,
-            )
+                negated_sum(0, CHUNK, partial[:])
 
-            if first + size == GAUSSIANS:
+            if k == CHUNKS_IN_BLOCK - 1:
                 nc.vector.tensor_tensor(
                     windows[b][:].indirect(offsets[:]), exponents[b][:], log_norm[:], ALU.add
                 )

@@ -17,8 +17,9 @@ CHUNK = 16
 CHUNKS_IN_BLOCK = GAUSSIANS // CHUNK
 CHUNKS = BLOCKS * CHUNKS_IN_BLOCK
 LOAD = 8
-GROUP = 8
-GPSIMD_SHARE = 5
+COLUMNS = 128
+GROUP = COLUMNS // CHUNK
+GPSIMD_SHARE = 6
 SMALL = 4
 PSUM_BANKS = 8
 
@@ -79,10 +80,11 @@ def tile_gaussiantensor_kernel(tc, base, x, means, offs, out):
                 pieces = [(nc.vector, x_psum[b], lo, lo + SMALL) for lo in range(0, CHUNK, SMALL)]
             else:
                 pieces = [
-                    (nc.vector, x_psum[b], 0, LOAD),
-                    (nc.vector, x_psum[b], LOAD, CHUNK - GPSIMD_SHARE),
-                    (nc.gpsimd, x_sbuf[b], CHUNK - GPSIMD_SHARE, CHUNK),
+                    (nc.gpsimd, x_sbuf[b], 0, GPSIMD_SHARE),
+                    (nc.vector, x_psum[b], GPSIMD_SHARE, LOAD),
+                    (nc.vector, x_psum[b], LOAD, CHUNK),
                 ]
+            on_tensor = LOAD if last_chunk else CHUNK
             diff = chunk.tile([P, CHUNK, VARIABLES], F32, name="diff")
             half_square = chunk.tile([P, CHUNK, VARIABLES], BF16, name="half_square")
             for engine, x_tile, lo, hi in pieces:
@@ -99,21 +101,21 @@ def tile_gaussiantensor_kernel(tc, base, x, means, offs, out):
                     ACT.Square,
                     scale=math.sqrt(0.5),
                 )
-                if last_chunk:
+                if lo >= on_tensor:
                     negated_sum(lo, hi, half_square[:, lo:hi, :])
 
-            if not last_chunk:
-                partial = psum.tile([P, CHUNK, GROUP], F32, name="partial")
-                groups = VARIABLES // GROUP
-                for g in range(groups):
-                    nc.tensor.matmul(
-                        partial[:],
-                        identity_bf16[:],
-                        half_square[:, :, g * GROUP : (g + 1) * GROUP],
-                        start=(g == 0),
-                        stop=(g == groups - 1),
-                    )
-                negated_sum(0, CHUNK, partial[:])
+            group = COLUMNS // on_tensor
+            partial = psum.tile([P, on_tensor, group], F32, name="partial")
+            groups = VARIABLES // group
+            for g in range(groups):
+                nc.tensor.matmul(
+                    partial[:],
+                    identity_bf16[:],
+                    half_square[:, :on_tensor, g * group : (g + 1) * group],
+                    start=(g == 0),
+                    stop=(g == groups - 1),
+                )
+            negated_sum(0, on_tensor, partial[:])
 
             if k == CHUNKS_IN_BLOCK - 1:
                 nc.vector.tensor_tensor(

@@ -22,6 +22,7 @@ GROUP = COLUMNS // CHUNK
 GPSIMD_SHARE = 6
 SMALL = 4
 PSUM_BANKS = 8
+PAIR = 2
 
 
 def tile_gaussiantensor_kernel(tc, base, x, means, offs, out):
@@ -31,31 +32,32 @@ def tile_gaussiantensor_kernel(tc, base, x, means, offs, out):
         tc.tile_pool(name="block", bufs=BLOCKS) as block,
         tc.tile_pool(name="load", bufs=CHUNKS * CHUNK // LOAD) as load,
         tc.tile_pool(name="chunk", bufs=CHUNKS) as chunk,
-        tc.psum_pool(name="psum", bufs=PSUM_BANKS - BLOCKS) as psum,
-        tc.psum_pool(name="psum_block", bufs=BLOCKS) as psum_block,
+        tc.psum_pool(name="psum", bufs=PSUM_BANKS - 1) as psum,
+        tc.psum_pool(name="psum_held", bufs=1) as psum_held,
     ):
         offsets = held.tile([P, GAUSSIANS // 16], U16, name="offsets")
-        nc.sync.dma_start(offsets[:], offs)
         log_norm = held.tile([P, GAUSSIANS], F32, name="log_norm")
         nc.vector.memset(log_norm[:], LOG_NORM)
         identity = held.tile([P, P], F32, name="identity")
         make_identity(nc, identity[:])
         identity_bf16 = held.tile([P, P], BF16, name="identity_bf16")
         make_identity(nc, identity_bf16[:])
+        half_identity = held.tile([P, P], BF16, name="half_identity")
+        nc.vector.tensor_scalar_mul(half_identity[:], identity_bf16[:], 0.5)
 
-        x_sbuf, x_psum, windows, exponents, loaded = [], [], [], [], []
-        for b in range(BLOCKS):
-            sample = block.tile([P, VARIABLES], F32, name="sample")
-            nc.sync.dma_start(sample[:], x[b * P : (b + 1) * P, :])
-            x_sbuf.append(sample)
-            sample_psum = psum_block.tile([P, VARIABLES], F32, name="sample_psum")
-            nc.tensor.matmul(sample_psum[:], identity[:], sample[:], start=True, stop=True)
-            x_psum.append(sample_psum)
+        windows, exponents, loaded = [], [], []
+        samples = held.tile([P, BLOCKS, VARIABLES], F32, name="samples")
+        nc.sync.dma_start(samples[:], x.rearrange("(b p) d -> p b d", p=P))
+        samples_psum = psum_held.tile([P, BLOCKS, VARIABLES], F32, name="samples_psum")
+        nc.tensor.matmul(samples_psum[:], identity[:], samples[:], start=True, stop=True)
+        x_sbuf = [samples[:, b, :] for b in range(BLOCKS)]
+        x_psum = [samples_psum[:, b, :] for b in range(BLOCKS)]
         for b in range(BLOCKS):
             for first in range(0, GAUSSIANS, LOAD):
                 mean = load.tile([P, LOAD, VARIABLES], F32, name="mean")
                 nc.sync.dma_start(mean[:], means[b * P : (b + 1) * P, first : first + LOAD, :])
                 loaded.append(mean)
+        nc.sync.dma_start(offsets[:], offs)
         for b in range(BLOCKS):
             window = block.tile([P, SLOTS], F32, name="window")
             nc.sync.dma_start(window[:], base[b * P : (b + 1) * P, :])
@@ -63,9 +65,37 @@ def tile_gaussiantensor_kernel(tc, base, x, means, offs, out):
             exponent = block.tile([P, GAUSSIANS], F32, name="exponent")
             exponents.append(exponent)
 
+        def scatter_and_store(b):
+            nc.vector.tensor_tensor(
+                windows[b][:].indirect(offsets[:]), exponents[b][:], log_norm[:], ALU.add
+            )
+            nc.sync.dma_start(out[b * P : (b + 1) * P, :], windows[b][:])
+
         for i in range(CHUNKS):
             b, k = divmod(i, CHUNKS_IN_BLOCK)
             last_chunk = i == CHUNKS - 1
+            diff = chunk.tile([P, CHUNK, VARIABLES], F32, name="diff")
+            paired = i < CHUNKS - PAIR
+            if paired and i % PAIR == 0:
+                pair_squared = chunk.tile([P, PAIR * CHUNK, VARIABLES], BF16, name="pair_squared")
+            if paired:
+                squared = pair_squared[:, i % PAIR * CHUNK : (i % PAIR + 1) * CHUNK, :]
+            else:
+                lone_squared = chunk.tile([P, CHUNK, VARIABLES], BF16, name="lone_squared")
+                squared = lone_squared[:]
+
+            def subtract(engine, x_tile, lo, hi):
+                engine.tensor_tensor(
+                    diff[:, lo:hi, :],
+                    loaded[(i * CHUNK + lo) // LOAD][:, lo % LOAD : lo % LOAD + hi - lo, :],
+                    x_tile.unsqueeze(1).to_broadcast([P, hi - lo, VARIABLES]),
+                    ALU.subtract,
+                )
+
+            def square(lo, hi, scale):
+                nc.scalar.activation(
+                    squared[:, lo:hi, :], diff[:, lo:hi, :], ACT.Square, scale=scale
+                )
 
             def negated_sum(lo, hi, summands):
                 nc.vector.tensor_reduce(
@@ -76,49 +106,50 @@ def tile_gaussiantensor_kernel(tc, base, x, means, offs, out):
                     negate=True,
                 )
 
-            if last_chunk:
-                pieces = [(nc.vector, x_psum[b], lo, lo + SMALL) for lo in range(0, CHUNK, SMALL)]
+            def sum_on_tensor(lo, hi, summands):
+                group = COLUMNS // (hi - lo)
+                partial = psum.tile([P, hi - lo, group], F32, name="partial")
+                groups = VARIABLES // group
+                for g in range(groups):
+                    nc.tensor.matmul(
+                        partial[:],
+                        half_identity[:],
+                        summands[:, :, g * group : (g + 1) * group],
+                        start=(g == 0),
+                        stop=(g == groups - 1),
+                    )
+                negated_sum(lo, hi, partial[:])
+
+            if paired:
+                subtract(nc.gpsimd, x_sbuf[b], 0, GPSIMD_SHARE)
+                square(0, GPSIMD_SHARE, 1.0)
+                subtract(nc.vector, x_psum[b], GPSIMD_SHARE, LOAD)
+                square(GPSIMD_SHARE, LOAD, 1.0)
+                subtract(nc.vector, x_psum[b], LOAD, CHUNK)
+                square(LOAD, CHUNK, 1.0)
+                if i % PAIR == PAIR - 1:
+                    sum_on_tensor(CHUNK - PAIR * CHUNK, CHUNK, pair_squared[:])
+            elif not last_chunk:
+                subtract(nc.vector, x_psum[b], 0, LOAD)
+                nc.gpsimd.tensor_tensor(
+                    squared[:, :GPSIMD_SHARE, :],
+                    diff[:, :GPSIMD_SHARE, :],
+                    diff[:, :GPSIMD_SHARE, :],
+                    ALU.mult,
+                )
+                square(GPSIMD_SHARE, LOAD, 1.0)
+                subtract(nc.vector, x_psum[b], LOAD, CHUNK)
+                square(LOAD, CHUNK, 1.0)
+                sum_on_tensor(0, CHUNK, squared)
             else:
-                pieces = [
-                    (nc.gpsimd, x_sbuf[b], 0, GPSIMD_SHARE),
-                    (nc.vector, x_psum[b], GPSIMD_SHARE, LOAD),
-                    (nc.vector, x_psum[b], LOAD, CHUNK),
-                ]
-            on_tensor = LOAD if last_chunk else CHUNK
-            diff = chunk.tile([P, CHUNK, VARIABLES], F32, name="diff")
-            half_square = chunk.tile([P, CHUNK, VARIABLES], BF16, name="half_square")
-            for engine, x_tile, lo, hi in pieces:
-                mean = loaded[(i * CHUNK + lo) // LOAD]
-                engine.tensor_tensor(
-                    diff[:, lo:hi, :],
-                    mean[:, lo % LOAD : lo % LOAD + hi - lo, :],
-                    x_tile[:].unsqueeze(1).to_broadcast([P, hi - lo, VARIABLES]),
-                    ALU.subtract,
-                )
-                nc.scalar.activation(
-                    half_square[:, lo:hi, :],
-                    diff[:, lo:hi, :],
-                    ACT.Square,
-                    scale=math.sqrt(0.5),
-                )
-                if lo >= on_tensor:
-                    negated_sum(lo, hi, half_square[:, lo:hi, :])
-
-            group = COLUMNS // on_tensor
-            partial = psum.tile([P, on_tensor, group], F32, name="partial")
-            groups = VARIABLES // group
-            for g in range(groups):
-                nc.tensor.matmul(
-                    partial[:],
-                    identity_bf16[:],
-                    half_square[:, :on_tensor, g * group : (g + 1) * group],
-                    start=(g == 0),
-                    stop=(g == groups - 1),
-                )
-            negated_sum(0, on_tensor, partial[:])
-
-            if k == CHUNKS_IN_BLOCK - 1:
-                nc.vector.tensor_tensor(
-                    windows[b][:].indirect(offsets[:]), exponents[b][:], log_norm[:], ALU.add
-                )
-                nc.sync.dma_start(out[b * P : (b + 1) * P, :], windows[b][:])
+                for lo in range(0, LOAD, SMALL):
+                    subtract(nc.vector, x_psum[b], lo, lo + SMALL)
+                    square(lo, lo + SMALL, 1.0)
+                for lo in range(LOAD, CHUNK, SMALL):
+                    subtract(nc.vector, x_psum[b], lo, lo + SMALL)
+                    square(lo, lo + SMALL, math.sqrt(0.5))
+                scatter_and_store(0)
+                for lo in range(LOAD, CHUNK, SMALL):
+                    negated_sum(lo, lo + SMALL, squared[:, lo : lo + SMALL, :])
+                sum_on_tensor(0, LOAD, squared[:, :LOAD, :])
+                scatter_and_store(1)

@@ -75,7 +75,7 @@ def tile_gaussiantensor_kernel(tc, base, x, means, offs, out):
             b, k = divmod(i, CHUNKS_IN_BLOCK)
             last_chunk = i == CHUNKS - 1
             diff = chunk.tile([P, CHUNK, VARIABLES], F32, name="diff")
-            paired = i < CHUNKS - PAIR
+            paired = b == 0
             if paired and i % PAIR == 0:
                 pair_squared = chunk.tile([P, PAIR * CHUNK, VARIABLES], BF16, name="pair_squared")
             if paired:

@@ -138,18 +138,17 @@ def tile_gaussiantensor_kernel(tc, base, x, means, offs, out):
                     ALU.mult,
                 )
                 square(GPSIMD_SHARE, LOAD, 1.0)
-                subtract(nc.vector, x_psum[b], LOAD, CHUNK)
-                square(LOAD, CHUNK, 1.0)
+                piece = SMALL if i == CHUNKS - 2 else LOAD
+                for lo in range(LOAD, CHUNK, piece):
+                    subtract(nc.vector, x_psum[b], lo, lo + piece)
+                    square(lo, lo + piece, 1.0)
                 sum_on_tensor(0, CHUNK, squared)
             else:
-                for lo in range(0, LOAD, SMALL):
+                for lo in range(0, CHUNK, SMALL):
                     subtract(nc.vector, x_psum[b], lo, lo + SMALL)
                     square(lo, lo + SMALL, 1.0)
-                for lo in range(LOAD, CHUNK, SMALL):
-                    subtract(nc.vector, x_psum[b], lo, lo + SMALL)
-                    square(lo, lo + SMALL, math.sqrt(0.5))
                 scatter_and_store(0)
-                for lo in range(LOAD, CHUNK, SMALL):
-                    negated_sum(lo, lo + SMALL, squared[:, lo : lo + SMALL, :])
                 sum_on_tensor(0, LOAD, squared[:, :LOAD, :])
+                for lo in range(LOAD, CHUNK, SMALL):
+                    sum_on_tensor(lo, lo + SMALL, squared[:, lo : lo + SMALL, :])
                 scatter_and_store(1)

import math

import concourse.mybir as mybir
from concourse.masks import make_identity

F32 = mybir.dt.float32
BF16 = mybir.dt.bfloat16
U16 = mybir.dt.uint16
ALU = mybir.AluOpType
ACT = mybir.ActivationFunctionType

P = 128
SAMPLES, SLOTS, GAUSSIANS, VARIABLES = 256, 512, 64, 64
BLOCKS = SAMPLES // P
LOG_NORM = -0.5 * VARIABLES * math.log(2.0 * math.pi)
CHUNK = 16
CHUNKS_IN_BLOCK = GAUSSIANS // CHUNK
CHUNKS = BLOCKS * CHUNKS_IN_BLOCK
LOAD = 8
COLUMNS = 128
GROUP = COLUMNS // CHUNK
GPSIMD_SHARE = 6
SMALL = 4
PSUM_BANKS = 8
PAIR = 2


def tile_gaussiantensor_kernel(tc, base, x, means, offs, out):
    nc = tc.nc
    with (
        tc.tile_pool(name="held", bufs=1) as held,
        tc.tile_pool(name="block", bufs=BLOCKS) as block,
        tc.tile_pool(name="load", bufs=CHUNKS * CHUNK // LOAD) as load,
        tc.tile_pool(name="chunk", bufs=CHUNKS) as chunk,
        tc.psum_pool(name="psum", bufs=PSUM_BANKS - 1) as psum,
        tc.psum_pool(name="psum_held", bufs=1) as psum_held,
    ):
        offsets = held.tile([P, GAUSSIANS // 16], U16, name="offsets")
        log_norm = held.tile([P, GAUSSIANS], F32, name="log_norm")
        nc.vector.memset(log_norm[:], LOG_NORM)
        identity = held.tile([P, P], F32, name="identity")
        make_identity(nc, identity[:])
        identity_bf16 = held.tile([P, P], BF16, name="identity_bf16")
        make_identity(nc, identity_bf16[:])
        half_identity = held.tile([P, P], BF16, name="half_identity")
        nc.vector.tensor_scalar_mul(half_identity[:], identity_bf16[:], 0.5)

        windows, exponents, loaded = [], [], []
        samples = held.tile([P, BLOCKS, VARIABLES], F32, name="samples")
        nc.sync.dma_start(samples[:], x.rearrange("(b p) d -> p b d", p=P))
        samples_psum = psum_held.tile([P, BLOCKS, VARIABLES], F32, name="samples_psum")
        nc.tensor.matmul(samples_psum[:], identity[:], samples[:], start=True, stop=True)
        x_sbuf = [samples[:, b, :] for b in range(BLOCKS)]
        x_psum = [samples_psum[:, b, :] for b in range(BLOCKS)]
        for b in range(BLOCKS):
            for first in range(0, GAUSSIANS, LOAD):
                mean = load.tile([P, LOAD, VARIABLES], F32, name="mean")
                nc.sync.dma_start(mean[:], means[b * P : (b + 1) * P, first : first + LOAD, :])
                loaded.append(mean)
        nc.sync.dma_start(offsets[:], offs)
        for b in range(BLOCKS):
            window = block.tile([P, SLOTS], F32, name="window")
            nc.sync.dma_start(window[:], base[b * P : (b + 1) * P, :])
            windows.append(window)
            exponent = block.tile([P, GAUSSIANS], F32, name="exponent")
            exponents.append(exponent)

        def scatter_and_store(b):
            nc.vector.tensor_tensor(
                windows[b][:].indirect(offsets[:]), exponents[b][:], log_norm[:], ALU.add
            )
            nc.sync.dma_start(out[b * P : (b + 1) * P, :], windows[b][:])

        for i in range(CHUNKS):
            b, k = divmod(i, CHUNKS_IN_BLOCK)
            last_chunk = i == CHUNKS - 1
            diff = chunk.tile([P, CHUNK, VARIABLES], F32, name="diff")
            paired = b == 0
            if paired and i % PAIR == 0:
                pair_squared = chunk.tile([P, PAIR * CHUNK, VARIABLES], BF16, name="pair_squared")
            if paired:
                squared = pair_squared[:, i % PAIR * CHUNK : (i % PAIR + 1) * CHUNK, :]
            else:
                lone_squared = chunk.tile([P, CHUNK, VARIABLES], BF16, name="lone_squared")
                squared = lone_squared[:]

            def subtract(engine, x_tile, lo, hi):
                engine.tensor_tensor(
                    diff[:, lo:hi, :],
                    loaded[(i * CHUNK + lo) // LOAD][:, lo % LOAD : lo % LOAD + hi - lo, :],
                    x_tile.unsqueeze(1).to_broadcast([P, hi - lo, VARIABLES]),
                    ALU.subtract,
                )

            def square(lo, hi, scale):
                nc.scalar.activation(
                    squared[:, lo:hi, :], diff[:, lo:hi, :], ACT.Square, scale=scale
                )

            def negated_sum(lo, hi, summands):
                nc.vector.tensor_reduce(
                    exponents[b][:, k * CHUNK + lo : k * CHUNK + hi],
                    summands,
                    axis=mybir.AxisListType.X,
                    op=ALU.add,
                    negate=True,
                )

            def sum_on_tensor(lo, hi, summands):
                group = COLUMNS // (hi - lo)
                partial = psum.tile([P, hi - lo, group], F32, name="partial")
                groups = VARIABLES // group
                for g in range(groups):
                    nc.tensor.matmul(
                        partial[:],
                        half_identity[:],
                        summands[:, :, g * group : (g + 1) * group],
                        start=(g == 0),
                        stop=(g == groups - 1),
                    )
                negated_sum(lo, hi, partial[:])

            if paired:
                subtract(nc.gpsimd, x_sbuf[b], 0, GPSIMD_SHARE)
                square(0, GPSIMD_SHARE, 1.0)
                subtract(nc.vector, x_psum[b], GPSIMD_SHARE, LOAD)
                square(GPSIMD_SHARE, LOAD, 1.0)
                subtract(nc.vector, x_psum[b], LOAD, CHUNK)
                square(LOAD, CHUNK, 1.0)
                if i % PAIR == PAIR - 1:
                    sum_on_tensor(CHUNK - PAIR * CHUNK, CHUNK, pair_squared[:])
            elif not last_chunk:
                subtract(nc.vector, x_psum[b], 0, LOAD)
                nc.gpsimd.tensor_tensor(
                    squared[:, :GPSIMD_SHARE, :],
                    diff[:, :GPSIMD_SHARE, :],
                    diff[:, :GPSIMD_SHARE, :],
                    ALU.mult,
                )
                square(GPSIMD_SHARE, LOAD, 1.0)
                piece = SMALL if i == CHUNKS - 2 else LOAD
                for lo in range(LOAD, CHUNK, piece):
                    subtract(nc.vector, x_psum[b], lo, lo + piece)
                    square(lo, lo + piece, 1.0)
                sum_on_tensor(0, CHUNK, squared)
            else:
                for lo in range(0, CHUNK, SMALL):
                    subtract(nc.vector, x_psum[b], lo, lo + SMALL)
                    square(lo, lo + SMALL, 1.0)
                scatter_and_store(0)
                sum_on_tensor(0, LOAD, squared[:, :LOAD, :])
                for lo in range(LOAD, CHUNK, SMALL):
                    sum_on_tensor(lo, lo + SMALL, squared[:, lo : lo + SMALL, :])
                scatter_and_store(1)
